import numpy as np
import ml_dtypes


def mxq(x, axis, fmt="e4m3"):
    dtype, down = {"e4m3": (ml_dtypes.float8_e4m3fn, 7), "e5m2": (ml_dtypes.float8_e5m2, 14)}[fmt]
    v = np.moveaxis(np.asarray(x, np.float32).astype(ml_dtypes.bfloat16).astype(np.float64), axis, -1)
    blocks = v.reshape(v.shape[:-1] + (-1, 32))
    amax = np.abs(blocks).max(-1, keepdims=True)
    byte = np.maximum(np.where(amax > 0, np.frexp(amax)[1] - 1 + 127, 0) - down, 1)
    scale = np.exp2(byte - 127.0)
    codes = (blocks / scale).astype(np.float32).astype(dtype).astype(np.float64)
    return np.moveaxis((codes * scale).reshape(v.shape), -1, axis)


WIDE = False


def mx_kscale(k):
    if not WIDE:
        return np.ones(k)
    levels = np.array([10, -10, 5, -5, 0])
    if k % 512:
        return np.exp2(np.random.permutation(np.resize(levels, k // 32))).repeat(32)
    a = np.empty((k // 512, 16))
    for p in range(k // 512):
        a[p, :8] = np.random.permutation(np.resize(levels, 8))
        for g in range(8):
            far = levels[np.abs(levels - a[p, g]) >= 10]
            a[p, g + 8] = far[np.random.randint(len(far))]
    return np.exp2(a.ravel()).repeat(32)


BF16 = ml_dtypes.bfloat16


def bf(x):
    return np.asarray(x, np.float32).astype(BF16)


def f64(x):
    return np.asarray(x).astype(np.float64)


B, L, D, H = 1, 4096, 512, 2
LN_EPS = 1e-5


def setup_inputs():
    s = mx_kscale(H * D)
    return {"heads": bf(np.random.standard_normal((H, L, D)) * 0.25 * s.reshape(H, D)[:, None, :]),
            "q": bf(np.random.standard_normal((B, L, D))),
            "proj_w": bf(np.random.standard_normal((D, H * D)) * 4.0 / np.sqrt(H * D) / s[None, :]),
            "proj_b": bf(np.random.standard_normal(D) * 0.1),
            "ln_gamma": bf(1.0 + np.random.standard_normal(D) * 0.1),
            "ln_beta": bf(np.random.standard_normal(D) * 0.1)}


def reference(heads, q, proj_w, proj_b, ln_gamma, ln_beta):
    hc = f64(heads).transpose(1, 0, 2).reshape(B, L, H * D)
    o = (mxq(hc, 2, "e4m3") @ mxq(f64(proj_w), 1, "e4m3").T) + f64(proj_b)
    x = o + f64(q)
    mu = x.mean(-1, keepdims=True)
    var = ((x - mu) ** 2).mean(-1, keepdims=True)
    return (x - mu) / np.sqrt(var + LN_EPS) * f64(ln_gamma) + f64(ln_beta)

@@ -1,0 +1,271 @@
+from contextlib import ExitStack
+
+import concourse.mybir as mybir
+from concourse.masks import make_identity
+
+F32 = mybir.dt.float32
+BF16 = mybir.dt.bfloat16
+U32 = mybir.dt.uint32
+U8 = mybir.dt.uint8
+FP8X4 = mybir.dt.float8_e4m3fn_x4
+ALU = mybir.AluOpType
+ACT = mybir.ActivationFunctionType
+
+P = 128
+HEADS = 2
+D = 512
+ROWS = 4096
+PACK = 4
+HALVES = 2
+TILES = 2
+UNITS_PER_GROUP = 2
+GROUP_TILES = TILES * UNITS_PER_GROUP
+GROUPS = ROWS // (P * GROUP_TILES)
+UNITS = GROUPS * UNITS_PER_GROUP
+W_TILES = D // P
+LN_EPS = 1e-5
+
+FLOPS = 2 * ROWS * HEADS * D * D
+
+
+def tile_multiheadattention_pb_t_kernel(
+    tc, heads, q, proj_w, proj_b, ln_gamma, ln_beta, out
+):
+    nc = tc.nc
+    heads_groups = heads.rearrange("h (g p t) d -> g p h (t d)", p=P, t=GROUP_TILES)
+    q_groups = q.flatten_outer_dims().rearrange("(g p t) d -> g p (t d)", p=P, t=GROUP_TILES)
+    out_groups = out.flatten_outer_dims().rearrange(
+        "(g p t) d -> g p (t d)", p=P, t=GROUP_TILES
+    )
+
+    with ExitStack() as stack:
+        const = stack.enter_context(tc.tile_pool(name="const", bufs=1))
+        heads_pool = stack.enter_context(tc.tile_pool(name="heads", bufs=3))
+        q_pool = stack.enter_context(tc.tile_pool(name="q", bufs=3))
+        resid_pool = stack.enter_context(tc.tile_pool(name="resid", bufs=4))
+        grouped_pool = stack.enter_context(tc.tile_pool(name="grouped", bufs=3))
+        mx_pool = stack.enter_context(tc.tile_pool(name="mx", bufs=3))
+        x_pool = stack.enter_context(tc.tile_pool(name="x", bufs=3))
+        y_pool = stack.enter_context(tc.tile_pool(name="y", bufs=4))
+        scratch_pool = stack.enter_context(tc.tile_pool(name="scratch", bufs=4))
+        stats_pool = stack.enter_context(tc.tile_pool(name="stats", bufs=4))
+        affine_psum = stack.enter_context(tc.psum_pool(name="affine_psum", bufs=1))
+        flip_psum = stack.enter_context(tc.psum_pool(name="flip_psum", bufs=3))
+        acc_psum = stack.enter_context(tc.psum_pool(name="acc_psum", bufs=2 * TILES))
+        stack.enter_context(tc.manual_schedule())
+
+        heads_sb, q_sb, resid, grouped, codes, scales = {}, {}, {}, {}, {}, {}
+        acc, x_sb, y_sb, row_sum, mean, rstd = {}, {}, {}, {}, {}, {}
+
+        def load(g, pieces):
+            heads_sb[g] = heads_pool.tile([P, HEADS, GROUP_TILES * D], BF16, name="heads_sb")
+            q_sb[g] = q_pool.tile([P, GROUP_TILES * D], BF16, name="q_sb")
+            width = GROUP_TILES * D // pieces
+            for piece in range(pieces):
+                cols = slice(piece * width, (piece + 1) * width)
+                nc.sync.dma_start(out=heads_sb[g][:, :, cols], in_=heads_groups[g][:, :, cols])
+                nc.sync.dma_start(out=q_sb[g][:, cols], in_=q_groups[g][:, cols])
+
+        def flip_rows(src_words, dst_words, copy):
+            flipped = flip_psum.tile([P, HEADS * HALVES * P], F32, tag="flipped")
+            planes = flipped[:].rearrange("p (h u r) -> p h u r", h=HEADS, u=HALVES)
+            for h in range(HEADS):
+                for u in range(HALVES):
+                    nc.tensor.transpose(planes[:, h, u, :], src_words[:, h, u, :], ident[:])
+            copy(out=dst_words, in_=planes.rearrange("p h u r -> p h r u"))
+
+        def flip_unit(unit):
+            g, part = divmod(unit, UNITS_PER_GROUP)
+            src = (
+                heads_sb[g][:]
+                .rearrange("p h x -> p (h x)")
+                .bitcast(F32)
+                .rearrange("p (h t w u) -> p h t u w", h=HEADS, t=GROUP_TILES, u=HALVES)
+            )
+            grouped[unit] = grouped_pool.tile(
+                [P, TILES * HEADS * P * PACK], BF16, name="grouped", align_bytes=64
+            )
+            dst = grouped[unit][:].bitcast(F32).rearrange(
+                "p (t h r u) -> p t h r u", t=TILES, h=HEADS, u=HALVES
+            )
+            for t in range(TILES):
+                flip_rows(src[:, :, part * TILES + t], dst[:, t], nc.scalar.copy)
+
+        def add_bias(unit):
+            g, part = divmod(unit, UNITS_PER_GROUP)
+            resid[unit] = resid_pool.tile([P, TILES, D], F32, name="resid")
+            nc.gpsimd.tensor_tensor(
+                out=resid[unit][:],
+                in0=q_sb[g][:, part * TILES * D : (part + 1) * TILES * D].rearrange(
+                    "p (t n) -> p t n", t=TILES
+                ),
+                in1=bias_sb[:].unsqueeze(1).to_broadcast([P, TILES, D]),
+                op=ALU.add,
+            )
+
+        def quantise(unit):
+            codes[unit] = mx_pool.tile([P, TILES * HEADS * P], U32, name="codes", align_bytes=64)
+            scales[unit] = mx_pool.tile([P, TILES * HEADS * P], U8, name="scales", align_bytes=64)
+            nc.vector.quantize_mx(
+                out=codes[unit][:].bitcast(FP8X4), scales=scales[unit][:], in_=grouped[unit][:]
+            )
+
+        def project(unit):
+            for t in range(TILES):
+                acc[unit, t] = acc_psum.tile([P, D], F32, name="acc")
+                for h in range(HEADS):
+                    rows = slice((t * HEADS + h) * P, (t * HEADS + h + 1) * P)
+                    cols = slice(h * D, (h + 1) * D)
+                    nc.tensor.matmul_mx(
+                        out=acc[unit, t][:],
+                        lhsT=codes[unit][:, rows].bitcast(FP8X4),
+                        lhsT_scale=scales[unit][:, rows],
+                        rhs=w_codes[:, cols].bitcast(FP8X4),
+                        rhs_scale=w_scales[:, cols],
+                        start=(h == 0),
+                        stop=(h == HEADS - 1),
+                    )
+
+        def add_residual(unit):
+            x_sb[unit] = x_pool.tile([P, TILES, D], F32, name="x_sb")
+            row_sum[unit] = stats_pool.tile([P, TILES], F32, name="row_sum")
+            for t in range(TILES):
+                nc.vector.scalar_tensor_tensor(
+                    out=x_sb[unit][:, t, :],
+                    in0=acc[unit, t][:],
+                    scalar=1.0,
+                    in1=resid[unit][:, t, :],
+                    op0=ALU.mult,
+                    op1=ALU.add,
+                    accum_out=row_sum[unit][:, t : t + 1],
+                )
+
+        def statistics(unit):
+            mean[unit] = stats_pool.tile([P, TILES], F32, name="mean")
+            nc.scalar.mul(out=mean[unit][:], in_=row_sum[unit][:], mul=1.0 / D)
+            sq_sum = stats_pool.tile([P, TILES], F32, name="sq_sum")
+            for t in range(TILES):
+                squares = scratch_pool.tile([P, D], BF16, name="squares")
+                nc.scalar.activation(
+                    out=squares[:],
+                    in_=x_sb[unit][:, t, :],
+                    func=ACT.Square,
+                    bias=mean[unit][:, t : t + 1],
+                    scale=-1.0,
+                    accum_out=sq_sum[:, t : t + 1],
+                )
+            rstd[unit] = stats_pool.tile([P, TILES], F32, name="rstd")
+            nc.scalar.activation(
+                out=rstd[unit][:],
+                in_=sq_sum[:],
+                func=ACT.Abs_reciprocal_sqrt,
+                bias=eps[:],
+                scale=1.0 / D,
+            )
+
+        def centre(unit):
+            y_sb[unit] = y_pool.tile([P, TILES, D], F32, name="y_sb")
+            for t in range(TILES):
+                nc.vector.scalar_tensor_tensor(
+                    out=y_sb[unit][:, t, :],
+                    in0=x_sb[unit][:, t, :],
+                    scalar=mean[unit][:, t : t + 1],
+                    in1=gamma_bc,
+                    op0=ALU.subtract,
+                    op1=ALU.mult,
+                )
+
+        def finish(unit):
+            g, part = divmod(unit, UNITS_PER_GROUP)
+            for t in range(TILES):
+                nc.vector.scalar_tensor_tensor(
+                    out=y_sb[unit][:, t, :],
+                    in0=y_sb[unit][:, t, :],
+                    scalar=rstd[unit][:, t : t + 1],
+                    in1=beta_bc,
+                    op0=ALU.mult,
+                    op1=ALU.add,
+                )
+            nc.sync.dma_start(
+                out=out_groups[g][:, part * TILES * D : (part + 1) * TILES * D],
+                in_=y_sb[unit][:].rearrange("p t n -> p (t n)"),
+            )
+
+        ident = const.tile([P, P], F32)
+        make_identity(nc, ident[:])
+        ones = const.tile([P, P], BF16)
+        nc.vector.memset(ones[:], 1.0)
+        eps = const.tile([P, 1], F32)
+        nc.vector.memset(eps[:], LN_EPS)
+        vec_rows = const.tile([P, 3 * D], BF16)
+        nc.vector.memset(vec_rows[:], 0.0)
+        warm = const.tile([P, 1], F32)
+        nc.scalar.activation(out=warm[:], in_=eps[:], func=ACT.Abs_reciprocal_sqrt)
+
+        w_raw = const.tile([P, W_TILES, HEADS * D], BF16)
+        w_rows = proj_w.rearrange("(j p) k -> p j k", p=P)
+        for half in range(2):
+            js = slice(half * W_TILES // 2, (half + 1) * W_TILES // 2)
+            nc.sync.dma_start(out=w_raw[:, js, :], in_=w_rows[:, js, :])
+        for i, vec in enumerate((proj_b, ln_gamma, ln_beta)):
+            nc.sync.dma_start(out=vec_rows[0:1, i * D : (i + 1) * D], in_=vec.unsqueeze(0))
+        load(0, pieces=UNITS_PER_GROUP)
+        load(1, pieces=1)
+
+        w_words = (
+            w_raw[:]
+            .rearrange("p j k -> p (j k)")
+            .bitcast(F32)
+            .rearrange("p (j h w u) -> p j h u w", j=W_TILES, h=HEADS, u=HALVES)
+        )
+        w_grouped = const.tile([P, HEADS * D * PACK], BF16, align_bytes=64)
+        w_grouped_words = w_grouped[:].bitcast(F32).rearrange(
+            "p (h n u) -> p h n u", h=HEADS, u=HALVES
+        )
+        for j in range(W_TILES):
+            flip_rows(
+                w_words[:, j],
+                w_grouped_words[:, :, j * P : (j + 1) * P, :],
+                nc.vector.tensor_copy if j % 2 == 0 else nc.scalar.copy,
+            )
+
+        bias_ps = flip_psum.tile([P, D], F32, tag="flipped")
+        nc.tensor.matmul(out=bias_ps[:], lhsT=ones[:], rhs=vec_rows[:, 0:D], start=True, stop=True)
+        bias_sb = const.tile([P, D], F32)
+        nc.vector.tensor_copy(out=bias_sb[:], in_=bias_ps[:])
+        affine = affine_psum.tile([P, 2 * D], BF16)
+        for i in range(2):
+            nc.tensor.matmul(
+                out=affine[:, i * D : (i + 1) * D],
+                lhsT=ones[:],
+                rhs=vec_rows[:, (i + 1) * D : (i + 2) * D],
+                start=True,
+                stop=True,
+            )
+        gamma_bc = affine[:, 0:D]
+        beta_bc = affine[:, D : 2 * D]
+
+        w_codes = const.tile([P, HEADS * D], U32, align_bytes=64)
+        w_scales = const.tile([P, HEADS * D], U8, align_bytes=64)
+        nc.vector.quantize_mx(
+            out=w_codes[:].bitcast(FP8X4), scales=w_scales[:], in_=w_grouped[:]
+        )
+
+        for unit in range(-2, UNITS + 1):
+            ahead = unit + 2
+            if ahead % UNITS_PER_GROUP == 0 and ahead // UNITS_PER_GROUP + 2 < GROUPS:
+                load(ahead // UNITS_PER_GROUP + 2, pieces=1)
+            if ahead < UNITS:
+                flip_unit(ahead)
+                add_bias(ahead)
+            if 0 <= unit < UNITS:
+                add_residual(unit)
+            if 0 <= unit + 1 < UNITS:
+                quantise(unit + 1)
+                project(unit + 1)
+            if 0 <= unit < UNITS:
+                statistics(unit)
+            if 0 <= unit - 1:
+                finish(unit - 1)
+            if 0 <= unit < UNITS:
+                centre(unit)

@@ -93,6 +93,9 @@ def tile_multiheadattention_pb_t_kernel(
 
         def add_bias(unit):
             g, part = divmod(unit, UNITS_PER_GROUP)
+            if unit - 1 in codes:
+                gate = stats_pool.tile([P, 1], U32, name="gate")
+                nc.gpsimd.tensor_copy(out=gate[:], in_=codes[unit - 1][:, 0:1])
             resid[unit] = resid_pool.tile([P, TILES, D], F32, name="resid")
             nc.gpsimd.tensor_tensor(
                 out=resid[unit][:],
@@ -257,12 +260,13 @@ def tile_multiheadattention_pb_t_kernel(
                 load(ahead // UNITS_PER_GROUP + 2, pieces=1)
             if ahead < UNITS:
                 flip_unit(ahead)
-                add_bias(ahead)
             if 0 <= unit < UNITS:
                 add_residual(unit)
             if 0 <= unit + 1 < UNITS:
                 quantise(unit + 1)
                 project(unit + 1)
+            if ahead < UNITS:
+                add_bias(ahead)
             if 0 <= unit < UNITS:
                 statistics(unit)
             if 0 <= unit - 1:

@@ -24,6 +24,8 @@ GROUPS = ROWS // (P * GROUP_TILES)
 UNITS = GROUPS * UNITS_PER_GROUP
 W_TILES = D // P
 LN_EPS = 1e-5
+HELPED = frozenset(u for u in range(2, UNITS) if u % 4 != 0)
+OFFLOADED = HELPED - {UNITS - 1}
 
 FLOPS = 2 * ROWS * HEADS * D * D
 
@@ -54,25 +56,32 @@ def tile_multiheadattention_pb_t_kernel(
         acc_psum = stack.enter_context(tc.psum_pool(name="acc_psum", bufs=2 * TILES))
         stack.enter_context(tc.manual_schedule())
 
-        heads_sb, q_sb, resid, grouped, codes, scales = {}, {}, {}, {}, {}, {}
-        acc, x_sb, y_sb, row_sum, mean, rstd = {}, {}, {}, {}, {}, {}
+        heads_sb, q_sb, resid, flipped, grouped, codes, scales = {}, {}, {}, {}, {}, {}, {}
+        total, acc, x_sb, y_sb = {}, {}, {}, {}
+        row_sum, mean, sq_sum, rstd = {}, {}, {}, {}
 
-        def load(g, pieces):
+        def load(g, heads_pieces, q_pieces):
             heads_sb[g] = heads_pool.tile([P, HEADS, GROUP_TILES * D], BF16, name="heads_sb")
             q_sb[g] = q_pool.tile([P, GROUP_TILES * D], BF16, name="q_sb")
-            width = GROUP_TILES * D // pieces
-            for piece in range(pieces):
-                cols = slice(piece * width, (piece + 1) * width)
+            heads_at = 0
+            q_at = {sum(q_pieces[:i]): tiles for i, tiles in enumerate(q_pieces)}
+            for tiles in heads_pieces:
+                cols = slice(heads_at * D, (heads_at + tiles) * D)
                 nc.sync.dma_start(out=heads_sb[g][:, :, cols], in_=heads_groups[g][:, :, cols])
-                nc.sync.dma_start(out=q_sb[g][:, cols], in_=q_groups[g][:, cols])
+                if heads_at in q_at:
+                    cols = slice(heads_at * D, (heads_at + q_at[heads_at]) * D)
+                    nc.sync.dma_start(out=q_sb[g][:, cols], in_=q_groups[g][:, cols])
+                heads_at += tiles
 
-        def flip_rows(src_words, dst_words, copy):
-            flipped = flip_psum.tile([P, HEADS * HALVES * P], F32, tag="flipped")
+        def flip_rows(flipped, src_words):
             planes = flipped[:].rearrange("p (h u r) -> p h u r", h=HEADS, u=HALVES)
             for h in range(HEADS):
                 for u in range(HALVES):
                     nc.tensor.transpose(planes[:, h, u, :], src_words[:, h, u, :], ident[:])
-            copy(out=dst_words, in_=planes.rearrange("p h u r -> p h r u"))
+
+        def copy_flipped(flipped, dst_words, copy):
+            planes = flipped[:].rearrange("p (h u r) -> p h r u", h=HEADS, u=HALVES)
+            copy(out=dst_words, in_=planes)
 
         def flip_unit(unit):
             g, part = divmod(unit, UNITS_PER_GROUP)
@@ -82,29 +91,53 @@ def tile_multiheadattention_pb_t_kernel(
                 .bitcast(F32)
                 .rearrange("p (h t w u) -> p h t u w", h=HEADS, t=GROUP_TILES, u=HALVES)
             )
-            grouped[unit] = grouped_pool.tile(
-                [P, TILES * HEADS * P * PACK], BF16, name="grouped", align_bytes=64
-            )
+            for t in range(TILES):
+                flipped[unit, t] = flip_psum.tile([P, D], F32, name="flipped")
+                flip_rows(flipped[unit, t], src[:, :, part * TILES + t])
+
+        def copy_tile(unit, t):
+            if t == 0:
+                grouped[unit] = grouped_pool.tile(
+                    [P, TILES * HEADS * P * PACK], BF16, name="grouped", align_bytes=64
+                )
             dst = grouped[unit][:].bitcast(F32).rearrange(
                 "p (t h r u) -> p t h r u", t=TILES, h=HEADS, u=HALVES
             )
-            for t in range(TILES):
-                flip_rows(src[:, :, part * TILES + t], dst[:, t], nc.scalar.copy)
+            copy_flipped(flipped[unit, t], dst[:, t], nc.scalar.copy)
 
-        def add_bias(unit):
+        def q_rows(unit):
             g, part = divmod(unit, UNITS_PER_GROUP)
-            if unit - 1 in codes:
-                gate = stats_pool.tile([P, 1], U32, name="gate")
-                nc.gpsimd.tensor_copy(out=gate[:], in_=codes[unit - 1][:, 0:1])
+            rows = q_sb[g][:].rearrange("p (t n) -> p t n", t=GROUP_TILES)
+            return rows[:, part * TILES : (part + 1) * TILES, :]
+
+        def sum_first_residual(unit):
             resid[unit] = resid_pool.tile([P, TILES, D], F32, name="resid")
+            if unit in HELPED:
+                bank = flip_psum.tile([P, D], F32, name="flipped")
+                nc.tensor.matmul(
+                    out=bank[:], lhsT=ident_bf[:], rhs=q_rows(unit)[:, 0, :], start=True, stop=False
+                )
+                nc.tensor.matmul(
+                    out=bank[:], lhsT=ones[:], rhs=vec_rows[:, 0:D], start=False, stop=True
+                )
+                total[unit] = bank
+
+        def copy_first_residual(unit):
+            if unit in HELPED:
+                nc.scalar.copy(out=resid[unit][:, 0, :], in_=total[unit][:])
+
+        def add_residuals(unit):
+            first = 1 if unit in HELPED else 0
             nc.gpsimd.tensor_tensor(
-                out=resid[unit][:],
-                in0=q_sb[g][:, part * TILES * D : (part + 1) * TILES * D].rearrange(
-                    "p (t n) -> p t n", t=TILES
-                ),
-                in1=bias_sb[:].unsqueeze(1).to_broadcast([P, TILES, D]),
+                out=resid[unit][:, first:, :],
+                in0=q_rows(unit)[:, first:, :],
+                in1=bias_sb[:].unsqueeze(1).to_broadcast([P, TILES - first, D]),
                 op=ALU.add,
             )
+
+        def wait_for_codes(unit):
+            gate = stats_pool.tile([P, 1], U32, name="gate")
+            nc.gpsimd.tensor_copy(out=gate[:], in_=codes[unit][:, 0:1])
 
         def quantise(unit):
             codes[unit] = mx_pool.tile([P, TILES * HEADS * P], U32, name="codes", align_bytes=64)
@@ -143,10 +176,12 @@ def tile_multiheadattention_pb_t_kernel(
                     accum_out=row_sum[unit][:, t : t + 1],
                 )
 
-        def statistics(unit):
+        def average(unit):
             mean[unit] = stats_pool.tile([P, TILES], F32, name="mean")
             nc.scalar.mul(out=mean[unit][:], in_=row_sum[unit][:], mul=1.0 / D)
-            sq_sum = stats_pool.tile([P, TILES], F32, name="sq_sum")
+
+        def sum_squares(unit):
+            sq_sum[unit] = stats_pool.tile([P, TILES], F32, name="sq_sum")
             for t in range(TILES):
                 squares = scratch_pool.tile([P, D], BF16, name="squares")
                 nc.scalar.activation(
@@ -155,12 +190,14 @@ def tile_multiheadattention_pb_t_kernel(
                     func=ACT.Square,
                     bias=mean[unit][:, t : t + 1],
                     scale=-1.0,
-                    accum_out=sq_sum[:, t : t + 1],
+                    accum_out=sq_sum[unit][:, t : t + 1],
                 )
+
+        def invert_deviation(unit):
             rstd[unit] = stats_pool.tile([P, TILES], F32, name="rstd")
             nc.scalar.activation(
                 out=rstd[unit][:],
-                in_=sq_sum[:],
+                in_=sq_sum[unit][:],
                 func=ACT.Abs_reciprocal_sqrt,
                 bias=eps[:],
                 scale=1.0 / D,
@@ -178,9 +215,17 @@ def tile_multiheadattention_pb_t_kernel(
                     op1=ALU.mult,
                 )
 
-        def finish(unit):
+        def store(unit, first, tiles):
             g, part = divmod(unit, UNITS_PER_GROUP)
-            for t in range(TILES):
+            row = part * TILES + first
+            nc.sync.dma_start(
+                out=out_groups[g][:, row * D : (row + tiles) * D],
+                in_=y_sb[unit][:, first : first + tiles, :].rearrange("p t n -> p (t n)"),
+            )
+
+        def finish(unit):
+            tiles = TILES - 1 if unit in OFFLOADED else TILES
+            for t in range(tiles):
                 nc.vector.scalar_tensor_tensor(
                     out=y_sb[unit][:, t, :],
                     in0=y_sb[unit][:, t, :],
@@ -189,31 +234,48 @@ def tile_multiheadattention_pb_t_kernel(
                     op0=ALU.mult,
                     op1=ALU.add,
                 )
-            nc.sync.dma_start(
-                out=out_groups[g][:, part * TILES * D : (part + 1) * TILES * D],
-                in_=y_sb[unit][:].rearrange("p t n -> p (t n)"),
+                if unit == UNITS - 1:
+                    store(unit, t, 1)
+            if unit < UNITS - 1:
+                store(unit, 0, tiles)
+
+        def scale_last(unit):
+            t = TILES - 1
+            nc.scalar.activation(
+                out=y_sb[unit][:, t, :],
+                in_=y_sb[unit][:, t, :],
+                func=ACT.Copy,
+                scale=rstd[unit][:, t : t + 1],
             )
 
+        def shift_last(unit):
+            t = TILES - 1
+            nc.gpsimd.tensor_tensor(
+                out=y_sb[unit][:, t, :], in0=y_sb[unit][:, t, :], in1=beta_sb[:], op=ALU.add
+            )
+
+        vec_rows = const.tile([P, 3 * D], BF16)
+        nc.vector.memset(vec_rows[:].bitcast(F32), 0.0)
         ident = const.tile([P, P], F32)
         make_identity(nc, ident[:])
         ones = const.tile([P, P], BF16)
         nc.vector.memset(ones[:], 1.0)
         eps = const.tile([P, 1], F32)
         nc.vector.memset(eps[:], LN_EPS)
-        vec_rows = const.tile([P, 3 * D], BF16)
-        nc.vector.memset(vec_rows[:], 0.0)
-        warm = const.tile([P, 1], F32)
-        nc.scalar.activation(out=warm[:], in_=eps[:], func=ACT.Abs_reciprocal_sqrt)
+        ident_bf = const.tile([P, P], BF16)
+        nc.vector.tensor_copy(out=ident_bf[:], in_=ident[:])
 
+        for i, vec in enumerate((proj_b, ln_gamma, ln_beta)):
+            nc.scalar.dma_start(out=vec_rows[0:1, i * D : (i + 1) * D], in_=vec.unsqueeze(0))
         w_raw = const.tile([P, W_TILES, HEADS * D], BF16)
         w_rows = proj_w.rearrange("(j p) k -> p j k", p=P)
-        for half in range(2):
-            js = slice(half * W_TILES // 2, (half + 1) * W_TILES // 2)
-            nc.sync.dma_start(out=w_raw[:, js, :], in_=w_rows[:, js, :])
-        for i, vec in enumerate((proj_b, ln_gamma, ln_beta)):
-            nc.sync.dma_start(out=vec_rows[0:1, i * D : (i + 1) * D], in_=vec.unsqueeze(0))
-        load(0, pieces=UNITS_PER_GROUP)
-        load(1, pieces=1)
+        for j in range(W_TILES):
+            nc.sync.dma_start(out=w_raw[:, j, :], in_=w_rows[:, j, :])
+        load(0, heads_pieces=(TILES, TILES), q_pieces=(TILES, TILES))
+        load(1, heads_pieces=(GROUP_TILES,), q_pieces=(GROUP_TILES,))
+        load(2, heads_pieces=(GROUP_TILES,), q_pieces=(GROUP_TILES,))
+        warm = const.tile([P, 1], F32)
+        nc.scalar.activation(out=warm[:], in_=eps[:], func=ACT.Abs_reciprocal_sqrt)
 
         w_words = (
             w_raw[:]
@@ -226,50 +288,93 @@ def tile_multiheadattention_pb_t_kernel(
             "p (h n u) -> p h n u", h=HEADS, u=HALVES
         )
         for j in range(W_TILES):
-            flip_rows(
-                w_words[:, j],
+            bank = acc_psum.tile([P, D], F32, name="acc")
+            flip_rows(bank, w_words[:, j])
+            copy_flipped(
+                bank,
                 w_grouped_words[:, :, j * P : (j + 1) * P, :],
                 nc.vector.tensor_copy if j % 2 == 0 else nc.scalar.copy,
             )
-
-        bias_ps = flip_psum.tile([P, D], F32, tag="flipped")
-        nc.tensor.matmul(out=bias_ps[:], lhsT=ones[:], rhs=vec_rows[:, 0:D], start=True, stop=True)
-        bias_sb = const.tile([P, D], F32)
-        nc.vector.tensor_copy(out=bias_sb[:], in_=bias_ps[:])
-        affine = affine_psum.tile([P, 2 * D], BF16)
-        for i in range(2):
-            nc.tensor.matmul(
-                out=affine[:, i * D : (i + 1) * D],
-                lhsT=ones[:],
-                rhs=vec_rows[:, (i + 1) * D : (i + 2) * D],
-                start=True,
-                stop=True,
-            )
-        gamma_bc = affine[:, 0:D]
-        beta_bc = affine[:, D : 2 * D]
-
+        flip_unit(0)
+        for t in range(TILES):
+            copy_tile(0, t)
         w_codes = const.tile([P, HEADS * D], U32, align_bytes=64)
         w_scales = const.tile([P, HEADS * D], U8, align_bytes=64)
         nc.vector.quantize_mx(
             out=w_codes[:].bitcast(FP8X4), scales=w_scales[:], in_=w_grouped[:]
         )
+        def broadcast(bank, i):
+            nc.tensor.matmul(
+                out=bank,
+                lhsT=ones[:],
+                rhs=vec_rows[:, i * D : (i + 1) * D],
+                start=True,
+                stop=True,
+            )
 
-        for unit in range(-2, UNITS + 1):
+        bias_ps = flip_psum.tile([P, D], F32, name="flipped")
+        broadcast(bias_ps[:], 0)
+        flip_unit(1)
+        for t in range(TILES):
+            copy_tile(1, t)
+        sum_first_residual(1)
+        quantise(0)
+        project(0)
+        resid[0] = resid_pool.tile([P, TILES, D], F32, name="resid")
+        for t in range(TILES):
+            nc.vector.tensor_tensor(
+                out=resid[0][:, t, :], in0=q_rows(0)[:, t, :], in1=bias_ps[:], op=ALU.add
+            )
+        bias_sb = const.tile([P, D], F32)
+        nc.scalar.copy(out=bias_sb[:], in_=bias_ps[:])
+        wait_for_codes(0)
+        add_residuals(1)
+        affine = affine_psum.tile([P, 2 * D], BF16)
+        gamma_bc = affine[:, 0:D]
+        beta_bc = affine[:, D : 2 * D]
+        broadcast(gamma_bc, 1)
+        broadcast(beta_bc, 2)
+        beta_sb = const.tile([P, D], BF16)
+        nc.scalar.copy(out=beta_sb[:], in_=beta_bc)
+
+        for unit in range(UNITS + 1):
             ahead = unit + 2
             if ahead % UNITS_PER_GROUP == 0 and ahead // UNITS_PER_GROUP + 2 < GROUPS:
-                load(ahead // UNITS_PER_GROUP + 2, pieces=1)
+                load(ahead // UNITS_PER_GROUP + 2, heads_pieces=(GROUP_TILES,), q_pieces=(GROUP_TILES,))
             if ahead < UNITS:
                 flip_unit(ahead)
-            if 0 <= unit < UNITS:
-                add_residual(unit)
-            if 0 <= unit + 1 < UNITS:
+                sum_first_residual(ahead)
+            if unit + 1 == UNITS - 1:
                 quantise(unit + 1)
                 project(unit + 1)
+            if unit < UNITS:
+                add_residual(unit)
             if ahead < UNITS:
-                add_bias(ahead)
-            if 0 <= unit < UNITS:
-                statistics(unit)
+                copy_tile(ahead, 0)
+            if unit - 1 in OFFLOADED:
+                scale_last(unit - 1)
+            if unit < UNITS:
+                average(unit)
+            if ahead < UNITS:
+                copy_tile(ahead, 1)
+            if unit < UNITS:
+                sum_squares(unit)
+            if ahead < UNITS:
+                copy_first_residual(ahead)
+            if unit < UNITS:
+                invert_deviation(unit)
+            if unit + 1 < UNITS - 1:
+                quantise(unit + 1)
+                project(unit + 1)
+            if unit + 1 < UNITS:
+                wait_for_codes(unit + 1)
+            if unit - 1 in OFFLOADED:
+                shift_last(unit - 1)
+            if ahead < UNITS:
+                add_residuals(ahead)
             if 0 <= unit - 1:
                 finish(unit - 1)
-            if 0 <= unit < UNITS:
+            if unit - 1 in OFFLOADED:
+                store(unit - 1, TILES - 1, 1)
+            if unit < UNITS:
                 centre(unit)

@@ -25,7 +25,7 @@ UNITS = GROUPS * UNITS_PER_GROUP
 W_TILES = D // P
 LN_EPS = 1e-5
 HELPED = frozenset(u for u in range(2, UNITS) if u % 4 != 0)
-OFFLOADED = HELPED - {UNITS - 1}
+OFFLOADED = frozenset(range(UNITS - 1))
 
 FLOPS = 2 * ROWS * HEADS * D * D
 
@@ -368,10 +368,10 @@ def tile_multiheadattention_pb_t_kernel(
                 project(unit + 1)
             if unit + 1 < UNITS:
                 wait_for_codes(unit + 1)
-            if unit - 1 in OFFLOADED:
-                shift_last(unit - 1)
             if ahead < UNITS:
                 add_residuals(ahead)
+            if unit - 1 in OFFLOADED:
+                shift_last(unit - 1)
             if 0 <= unit - 1:
                 finish(unit - 1)
             if unit - 1 in OFFLOADED:

@@ -18,14 +18,12 @@ ROWS = 4096
 PACK = 4
 HALVES = 2
 TILES = 2
-UNITS_PER_GROUP = 2
-GROUP_TILES = TILES * UNITS_PER_GROUP
-GROUPS = ROWS // (P * GROUP_TILES)
-UNITS = GROUPS * UNITS_PER_GROUP
+UNITS = ROWS // (P * TILES)
+LOADED = 6
 W_TILES = D // P
 LN_EPS = 1e-5
 HELPED = frozenset(u for u in range(2, UNITS) if u % 4 != 0)
-OFFLOADED = frozenset(range(UNITS - 1))
+OFFLOADED = frozenset(u for u in range(UNITS - 1) if u + 3 in HELPED or u + 3 >= UNITS)
 
 FLOPS = 2 * ROWS * HEADS * D * D
 
@@ -34,16 +32,15 @@ def tile_multiheadattention_pb_t_kernel(
     tc, heads, q, proj_w, proj_b, ln_gamma, ln_beta, out
 ):
     nc = tc.nc
-    heads_groups = heads.rearrange("h (g p t) d -> g p h (t d)", p=P, t=GROUP_TILES)
-    q_groups = q.flatten_outer_dims().rearrange("(g p t) d -> g p (t d)", p=P, t=GROUP_TILES)
-    out_groups = out.flatten_outer_dims().rearrange(
-        "(g p t) d -> g p (t d)", p=P, t=GROUP_TILES
-    )
+    heads_units = heads.rearrange("h (i p t) d -> i p h (t d)", p=P, t=TILES)
+    q_units = q.flatten_outer_dims().rearrange("(i p t) d -> i p (t d)", p=P, t=TILES)
+    out_units = out.flatten_outer_dims().rearrange("(i p t) d -> i p (t d)", p=P, t=TILES)
 
     with ExitStack() as stack:
         const = stack.enter_context(tc.tile_pool(name="const", bufs=1))
-        heads_pool = stack.enter_context(tc.tile_pool(name="heads", bufs=3))
-        q_pool = stack.enter_context(tc.tile_pool(name="q", bufs=3))
+        w_pool = stack.enter_context(tc.tile_pool(name="w", bufs=W_TILES))
+        heads_pool = stack.enter_context(tc.tile_pool(name="heads", bufs=LOADED))
+        q_pool = stack.enter_context(tc.tile_pool(name="q", bufs=LOADED))
         resid_pool = stack.enter_context(tc.tile_pool(name="resid", bufs=4))
         grouped_pool = stack.enter_context(tc.tile_pool(name="grouped", bufs=3))
         mx_pool = stack.enter_context(tc.tile_pool(name="mx", bufs=3))
@@ -60,18 +57,11 @@ def tile_multiheadattention_pb_t_kernel(
         total, acc, x_sb, y_sb = {}, {}, {}, {}
         row_sum, mean, sq_sum, rstd = {}, {}, {}, {}
 
-        def load(g, heads_pieces, q_pieces):
-            heads_sb[g] = heads_pool.tile([P, HEADS, GROUP_TILES * D], BF16, name="heads_sb")
-            q_sb[g] = q_pool.tile([P, GROUP_TILES * D], BF16, name="q_sb")
-            heads_at = 0
-            q_at = {sum(q_pieces[:i]): tiles for i, tiles in enumerate(q_pieces)}
-            for tiles in heads_pieces:
-                cols = slice(heads_at * D, (heads_at + tiles) * D)
-                nc.sync.dma_start(out=heads_sb[g][:, :, cols], in_=heads_groups[g][:, :, cols])
-                if heads_at in q_at:
-                    cols = slice(heads_at * D, (heads_at + q_at[heads_at]) * D)
-                    nc.sync.dma_start(out=q_sb[g][:, cols], in_=q_groups[g][:, cols])
-                heads_at += tiles
+        def load(unit):
+            heads_sb[unit] = heads_pool.tile([P, HEADS, TILES * D], BF16, name="heads_sb")
+            q_sb[unit] = q_pool.tile([P, TILES * D], BF16, name="q_sb")
+            nc.sync.dma_start(out=heads_sb[unit][:], in_=heads_units[unit])
+            nc.sync.dma_start(out=q_sb[unit][:], in_=q_units[unit])
 
         def flip_rows(flipped, src_words):
             planes = flipped[:].rearrange("p (h u r) -> p h u r", h=HEADS, u=HALVES)
@@ -83,17 +73,15 @@ def tile_multiheadattention_pb_t_kernel(
             planes = flipped[:].rearrange("p (h u r) -> p h r u", h=HEADS, u=HALVES)
             copy(out=dst_words, in_=planes)
 
-        def flip_unit(unit):
-            g, part = divmod(unit, UNITS_PER_GROUP)
+        def flip_tile(unit, t):
             src = (
-                heads_sb[g][:]
+                heads_sb[unit][:]
                 .rearrange("p h x -> p (h x)")
                 .bitcast(F32)
-                .rearrange("p (h t w u) -> p h t u w", h=HEADS, t=GROUP_TILES, u=HALVES)
+                .rearrange("p (h t w u) -> p h t u w", h=HEADS, t=TILES, u=HALVES)
             )
-            for t in range(TILES):
-                flipped[unit, t] = flip_psum.tile([P, D], F32, name="flipped")
-                flip_rows(flipped[unit, t], src[:, :, part * TILES + t])
+            flipped[unit, t] = flip_psum.tile([P, D], F32, name="flipped")
+            flip_rows(flipped[unit, t], src[:, :, t])
 
         def copy_tile(unit, t):
             if t == 0:
@@ -106,9 +94,7 @@ def tile_multiheadattention_pb_t_kernel(
             copy_flipped(flipped[unit, t], dst[:, t], nc.scalar.copy)
 
         def q_rows(unit):
-            g, part = divmod(unit, UNITS_PER_GROUP)
-            rows = q_sb[g][:].rearrange("p (t n) -> p t n", t=GROUP_TILES)
-            return rows[:, part * TILES : (part + 1) * TILES, :]
+            return q_sb[unit][:].rearrange("p (t n) -> p t n", t=TILES)
 
         def sum_first_residual(unit):
             resid[unit] = resid_pool.tile([P, TILES, D], F32, name="resid")
@@ -137,30 +123,35 @@ def tile_multiheadattention_pb_t_kernel(
 
         def wait_for_codes(unit):
             gate = stats_pool.tile([P, 1], U32, name="gate")
-            nc.gpsimd.tensor_copy(out=gate[:], in_=codes[unit][:, 0:1])
+            last = TILES * HEADS * P - 1
+            nc.gpsimd.tensor_copy(out=gate[:], in_=codes[unit][:, last : last + 1])
 
-        def quantise(unit):
-            codes[unit] = mx_pool.tile([P, TILES * HEADS * P], U32, name="codes", align_bytes=64)
-            scales[unit] = mx_pool.tile([P, TILES * HEADS * P], U8, name="scales", align_bytes=64)
+        def quantise(unit, first, count):
+            width = HEADS * P
+            if first == 0:
+                codes[unit] = mx_pool.tile([P, TILES * width], U32, name="codes", align_bytes=64)
+                scales[unit] = mx_pool.tile([P, TILES * width], U8, name="scales", align_bytes=64)
+            cols = slice(first * width, (first + count) * width)
             nc.vector.quantize_mx(
-                out=codes[unit][:].bitcast(FP8X4), scales=scales[unit][:], in_=grouped[unit][:]
+                out=codes[unit][:, cols].bitcast(FP8X4),
+                scales=scales[unit][:, cols],
+                in_=grouped[unit][:, first * width * PACK : (first + count) * width * PACK],
             )
 
-        def project(unit):
-            for t in range(TILES):
-                acc[unit, t] = acc_psum.tile([P, D], F32, name="acc")
-                for h in range(HEADS):
-                    rows = slice((t * HEADS + h) * P, (t * HEADS + h + 1) * P)
-                    cols = slice(h * D, (h + 1) * D)
-                    nc.tensor.matmul_mx(
-                        out=acc[unit, t][:],
-                        lhsT=codes[unit][:, rows].bitcast(FP8X4),
-                        lhsT_scale=scales[unit][:, rows],
-                        rhs=w_codes[:, cols].bitcast(FP8X4),
-                        rhs_scale=w_scales[:, cols],
-                        start=(h == 0),
-                        stop=(h == HEADS - 1),
-                    )
+        def project(unit, t):
+            acc[unit, t] = acc_psum.tile([P, D], F32, name="acc")
+            for h in range(HEADS):
+                rows = slice((t * HEADS + h) * P, (t * HEADS + h + 1) * P)
+                cols = slice(h * D, (h + 1) * D)
+                nc.tensor.matmul_mx(
+                    out=acc[unit, t][:],
+                    lhsT=codes[unit][:, rows].bitcast(FP8X4),
+                    lhsT_scale=scales[unit][:, rows],
+                    rhs=w_codes[:, cols].bitcast(FP8X4),
+                    rhs_scale=w_scales[:, cols],
+                    start=(h == 0),
+                    stop=(h == HEADS - 1),
+                )
 
         def add_residual(unit):
             x_sb[unit] = x_pool.tile([P, TILES, D], F32, name="x_sb")
@@ -216,10 +207,8 @@ def tile_multiheadattention_pb_t_kernel(
                 )
 
         def store(unit, first, tiles):
-            g, part = divmod(unit, UNITS_PER_GROUP)
-            row = part * TILES + first
             nc.sync.dma_start(
-                out=out_groups[g][:, row * D : (row + tiles) * D],
+                out=out_units[unit][:, first * D : (first + tiles) * D],
                 in_=y_sb[unit][:, first : first + tiles, :].rearrange("p t n -> p (t n)"),
             )
 
@@ -255,7 +244,7 @@ def tile_multiheadattention_pb_t_kernel(
             )
 
         vec_rows = const.tile([P, 3 * D], BF16)
-        nc.vector.memset(vec_rows[:].bitcast(F32), 0.0)
+        nc.gpsimd.memset(vec_rows[:].bitcast(F32), 0.0)
         ident = const.tile([P, P], F32)
         make_identity(nc, ident[:])
         ones = const.tile([P, P], BF16)
@@ -271,9 +260,8 @@ def tile_multiheadattention_pb_t_kernel(
         w_rows = proj_w.rearrange("(j p) k -> p j k", p=P)
         for j in range(W_TILES):
             nc.sync.dma_start(out=w_raw[:, j, :], in_=w_rows[:, j, :])
-        load(0, heads_pieces=(TILES, TILES), q_pieces=(TILES, TILES))
-        load(1, heads_pieces=(GROUP_TILES,), q_pieces=(GROUP_TILES,))
-        load(2, heads_pieces=(GROUP_TILES,), q_pieces=(GROUP_TILES,))
+        for unit in range(LOADED):
+            load(unit)
         warm = const.tile([P, 1], F32)
         nc.scalar.activation(out=warm[:], in_=eps[:], func=ACT.Abs_reciprocal_sqrt)
 
@@ -283,26 +271,30 @@ def tile_multiheadattention_pb_t_kernel(
             .bitcast(F32)
             .rearrange("p (j h w u) -> p j h u w", j=W_TILES, h=HEADS, u=HALVES)
         )
-        w_grouped = const.tile([P, HEADS * D * PACK], BF16, align_bytes=64)
-        w_grouped_words = w_grouped[:].bitcast(F32).rearrange(
-            "p (h n u) -> p h n u", h=HEADS, u=HALVES
-        )
-        for j in range(W_TILES):
-            bank = acc_psum.tile([P, D], F32, name="acc")
-            flip_rows(bank, w_words[:, j])
-            copy_flipped(
-                bank,
-                w_grouped_words[:, :, j * P : (j + 1) * P, :],
-                nc.vector.tensor_copy if j % 2 == 0 else nc.scalar.copy,
-            )
-        flip_unit(0)
-        for t in range(TILES):
-            copy_tile(0, t)
         w_codes = const.tile([P, HEADS * D], U32, align_bytes=64)
         w_scales = const.tile([P, HEADS * D], U8, align_bytes=64)
-        nc.vector.quantize_mx(
-            out=w_codes[:].bitcast(FP8X4), scales=w_scales[:], in_=w_grouped[:]
-        )
+        w_grouped = {}
+
+        def flip_weights(j):
+            bank = acc_psum.tile([P, D], F32, name="acc")
+            flip_rows(bank, w_words[:, j])
+            w_grouped[j] = w_pool.tile(
+                [P, HEADS * P * PACK], BF16, name="w_grouped", align_bytes=64
+            )
+            dst = w_grouped[j][:].bitcast(F32).rearrange(
+                "p (h n u) -> p h n u", h=HEADS, u=HALVES
+            )
+            copy_flipped(bank, dst, nc.vector.tensor_copy if j % 2 == 0 else nc.scalar.copy)
+
+        def quantise_weights(j):
+            for h in range(HEADS):
+                cols = slice(h * D + j * P, h * D + (j + 1) * P)
+                nc.vector.quantize_mx(
+                    out=w_codes[:, cols].bitcast(FP8X4),
+                    scales=w_scales[:, cols],
+                    in_=w_grouped[j][:, h * P * PACK : (h + 1) * P * PACK],
+                )
+
         def broadcast(bank, i):
             nc.tensor.matmul(
                 out=bank,
@@ -312,41 +304,52 @@ def tile_multiheadattention_pb_t_kernel(
                 stop=True,
             )
 
-        bias_ps = flip_psum.tile([P, D], F32, name="flipped")
+        flip_weights(0)
+        flip_weights(1)
+        quantise_weights(0)
+        flip_weights(2)
+        quantise_weights(1)
+        flip_weights(3)
+        quantise_weights(2)
+        quantise_weights(3)
+        bias_ps = acc_psum.tile([P, D], F32, name="acc")
         broadcast(bias_ps[:], 0)
-        flip_unit(1)
         for t in range(TILES):
+            flip_tile(0, t)
+            copy_tile(0, t)
+        for t in range(TILES):
+            flip_tile(1, t)
             copy_tile(1, t)
-        sum_first_residual(1)
-        quantise(0)
-        project(0)
-        resid[0] = resid_pool.tile([P, TILES, D], F32, name="resid")
-        for t in range(TILES):
-            nc.vector.tensor_tensor(
-                out=resid[0][:, t, :], in0=q_rows(0)[:, t, :], in1=bias_ps[:], op=ALU.add
-            )
-        bias_sb = const.tile([P, D], F32)
-        nc.scalar.copy(out=bias_sb[:], in_=bias_ps[:])
-        wait_for_codes(0)
-        add_residuals(1)
         affine = affine_psum.tile([P, 2 * D], BF16)
         gamma_bc = affine[:, 0:D]
         beta_bc = affine[:, D : 2 * D]
         broadcast(gamma_bc, 1)
         broadcast(beta_bc, 2)
+        resid[0] = resid_pool.tile([P, TILES, D], F32, name="resid")
+        for t in range(TILES):
+            nc.vector.tensor_tensor(
+                out=resid[0][:, t, :], in0=q_rows(0)[:, t, :], in1=bias_ps[:], op=ALU.add
+            )
+        for t in range(TILES):
+            quantise(0, t, 1)
+            project(0, t)
+        bias_sb = const.tile([P, D], F32)
+        nc.scalar.copy(out=bias_sb[:], in_=bias_ps[:])
         beta_sb = const.tile([P, D], BF16)
         nc.scalar.copy(out=beta_sb[:], in_=beta_bc)
+        sum_first_residual(1)
+        wait_for_codes(0)
+        add_residuals(1)
 
         for unit in range(UNITS + 1):
             ahead = unit + 2
-            if ahead % UNITS_PER_GROUP == 0 and ahead // UNITS_PER_GROUP + 2 < GROUPS:
-                load(ahead // UNITS_PER_GROUP + 2, heads_pieces=(GROUP_TILES,), q_pieces=(GROUP_TILES,))
+            after = unit + 1
+            if unit + LOADED < UNITS:
+                load(unit + LOADED)
             if ahead < UNITS:
-                flip_unit(ahead)
+                for t in range(TILES):
+                    flip_tile(ahead, t)
                 sum_first_residual(ahead)
-            if unit + 1 == UNITS - 1:
-                quantise(unit + 1)
-                project(unit + 1)
             if unit < UNITS:
                 add_residual(unit)
             if ahead < UNITS:
@@ -363,11 +366,11 @@ def tile_multiheadattention_pb_t_kernel(
                 copy_first_residual(ahead)
             if unit < UNITS:
                 invert_deviation(unit)
-            if unit + 1 < UNITS - 1:
-                quantise(unit + 1)
-                project(unit + 1)
-            if unit + 1 < UNITS:
-                wait_for_codes(unit + 1)
+            if after < UNITS:
+                quantise(after, 0, TILES)
+                for t in range(TILES):
+                    project(after, t)
+                wait_for_codes(after)
             if ahead < UNITS:
                 add_residuals(ahead)
             if unit - 1 in OFFLOADED:

@@ -275,16 +275,21 @@ def tile_multiheadattention_pb_t_kernel(
         w_scales = const.tile([P, HEADS * D], U8, align_bytes=64)
         w_grouped = {}
 
+        halves = {}
+        for j in range(W_TILES):
+            halves[j] = w_pool.tile([P, HEADS, HALVES, P], F32, name="halves")
+            nc.vector.tensor_copy(out=halves[j][:], in_=w_words[:, j])
+
         def flip_weights(j):
             bank = acc_psum.tile([P, D], F32, name="acc")
-            flip_rows(bank, w_words[:, j])
+            flip_rows(bank, halves[j][:])
             w_grouped[j] = w_pool.tile(
                 [P, HEADS * P * PACK], BF16, name="w_grouped", align_bytes=64
             )
             dst = w_grouped[j][:].bitcast(F32).rearrange(
                 "p (h n u) -> p h n u", h=HEADS, u=HALVES
             )
-            copy_flipped(bank, dst, nc.vector.tensor_copy if j % 2 == 0 else nc.scalar.copy)
+            copy_flipped(bank, dst, nc.vector.tensor_copy if j % 2 else nc.scalar.copy)
 
         def quantise_weights(j):
             for h in range(HEADS):
@@ -307,36 +312,36 @@ def tile_multiheadattention_pb_t_kernel(
         flip_weights(0)
         flip_weights(1)
         quantise_weights(0)
-        flip_weights(2)
         quantise_weights(1)
+        flip_weights(2)
         flip_weights(3)
         quantise_weights(2)
         quantise_weights(3)
+        flip_tile(0, 0)
+        copy_tile(0, 0)
         bias_ps = acc_psum.tile([P, D], F32, name="acc")
         broadcast(bias_ps[:], 0)
+        flip_tile(0, 1)
+        copy_tile(0, 1)
+        flip_tile(1, 0)
+        copy_tile(1, 0)
+        resid[0] = resid_pool.tile([P, TILES, D], F32, name="resid")
         for t in range(TILES):
-            flip_tile(0, t)
-            copy_tile(0, t)
-        for t in range(TILES):
-            flip_tile(1, t)
-            copy_tile(1, t)
+            quantise(0, t, 1)
+            project(0, t)
+            nc.vector.tensor_tensor(
+                out=resid[0][:, t, :], in0=q_rows(0)[:, t, :], in1=bias_ps[:], op=ALU.add
+            )
+        bias_sb = const.tile([P, D], F32)
+        nc.scalar.copy(out=bias_sb[:], in_=bias_ps[:])
+        flip_tile(1, 1)
+        copy_tile(1, 1)
         affine = affine_psum.tile([P, 2 * D], BF16)
         gamma_bc = affine[:, 0:D]
         beta_bc = affine[:, D : 2 * D]
         broadcast(gamma_bc, 1)
         broadcast(beta_bc, 2)
-        resid[0] = resid_pool.tile([P, TILES, D], F32, name="resid")
-        for t in range(TILES):
-            nc.vector.tensor_tensor(
-                out=resid[0][:, t, :], in0=q_rows(0)[:, t, :], in1=bias_ps[:], op=ALU.add
-            )
-        for t in range(TILES):
-            quantise(0, t, 1)
-            project(0, t)
-        bias_sb = const.tile([P, D], F32)
-        nc.scalar.copy(out=bias_sb[:], in_=bias_ps[:])
         beta_sb = const.tile([P, D], BF16)
-        nc.scalar.copy(out=beta_sb[:], in_=beta_bc)
         sum_first_residual(1)
         wait_for_codes(0)
         add_residuals(1)
@@ -352,11 +357,13 @@ def tile_multiheadattention_pb_t_kernel(
                 sum_first_residual(ahead)
             if unit < UNITS:
                 add_residual(unit)
+            if unit == 0:
+                average(unit)
             if ahead < UNITS:
                 copy_tile(ahead, 0)
             if unit - 1 in OFFLOADED:
                 scale_last(unit - 1)
-            if unit < UNITS:
+            if 0 < unit < UNITS:
                 average(unit)
             if ahead < UNITS:
                 copy_tile(ahead, 1)
@@ -371,6 +378,8 @@ def tile_multiheadattention_pb_t_kernel(
                 for t in range(TILES):
                     project(after, t)
                 wait_for_codes(after)
+            if unit == 0:
+                nc.vector.tensor_copy(out=beta_sb[:], in_=beta_bc)
             if ahead < UNITS:
                 add_residuals(ahead)
             if unit - 1 in OFFLOADED:

@@ -22,8 +22,10 @@ UNITS = ROWS // (P * TILES)
 LOADED = 6
 W_TILES = D // P
 LN_EPS = 1e-5
-HELPED = frozenset(u for u in range(2, UNITS) if u % 4 != 0)
-OFFLOADED = frozenset(u for u in range(UNITS - 1) if u + 3 in HELPED or u + 3 >= UNITS)
+HELPED = frozenset(range(3, UNITS)) - {UNITS // 2, 3 * UNITS // 4}
+OFFLOADED = frozenset(
+    (u, TILES - 1) for u in range(UNITS - 1) if u + 3 in HELPED or u + 3 >= UNITS
+) | {(UNITS - 3, 0)}
 
 FLOPS = 2 * ROWS * HEADS * D * D
 
@@ -167,9 +169,10 @@ def tile_multiheadattention_pb_t_kernel(
                     accum_out=row_sum[unit][:, t : t + 1],
                 )
 
-        def average(unit):
-            mean[unit] = stats_pool.tile([P, TILES], F32, name="mean")
-            nc.scalar.mul(out=mean[unit][:], in_=row_sum[unit][:], mul=1.0 / D)
+        def average(unit, tiles):
+            if tiles.start == 0:
+                mean[unit] = stats_pool.tile([P, TILES], F32, name="mean")
+            nc.scalar.mul(out=mean[unit][:, tiles], in_=row_sum[unit][:, tiles], mul=1.0 / D)
 
         def sum_squares(unit):
             sq_sum[unit] = stats_pool.tile([P, TILES], F32, name="sq_sum")
@@ -184,11 +187,12 @@ def tile_multiheadattention_pb_t_kernel(
                     accum_out=sq_sum[unit][:, t : t + 1],
                 )
 
-        def invert_deviation(unit):
-            rstd[unit] = stats_pool.tile([P, TILES], F32, name="rstd")
+        def invert_deviation(unit, tiles):
+            if tiles.start == 0:
+                rstd[unit] = stats_pool.tile([P, TILES], F32, name="rstd")
             nc.scalar.activation(
-                out=rstd[unit][:],
-                in_=sq_sum[unit][:],
+                out=rstd[unit][:, tiles],
+                in_=sq_sum[unit][:, tiles],
                 func=ACT.Abs_reciprocal_sqrt,
                 bias=eps[:],
                 scale=1.0 / D,
@@ -206,30 +210,26 @@ def tile_multiheadattention_pb_t_kernel(
                     op1=ALU.mult,
                 )
 
-        def store(unit, first, tiles):
+        def store(unit, t, cols):
             nc.sync.dma_start(
-                out=out_units[unit][:, first * D : (first + tiles) * D],
-                in_=y_sb[unit][:, first : first + tiles, :].rearrange("p t n -> p (t n)"),
+                out=out_units[unit][:, t * D + cols.start : t * D + cols.stop],
+                in_=y_sb[unit][:, t, cols],
             )
 
-        def finish(unit):
-            tiles = TILES - 1 if unit in OFFLOADED else TILES
-            for t in range(tiles):
+        def finish(unit, t, pieces):
+            for piece in range(pieces):
+                cols = slice(piece * D // pieces, (piece + 1) * D // pieces)
                 nc.vector.scalar_tensor_tensor(
-                    out=y_sb[unit][:, t, :],
-                    in0=y_sb[unit][:, t, :],
+                    out=y_sb[unit][:, t, cols],
+                    in0=y_sb[unit][:, t, cols],
                     scalar=rstd[unit][:, t : t + 1],
-                    in1=beta_bc,
+                    in1=beta_bc[:, cols],
                     op0=ALU.mult,
                     op1=ALU.add,
                 )
-                if unit == UNITS - 1:
-                    store(unit, t, 1)
-            if unit < UNITS - 1:
-                store(unit, 0, tiles)
+                store(unit, t, cols)
 
-        def scale_last(unit):
-            t = TILES - 1
+        def scale(unit, t):
             nc.scalar.activation(
                 out=y_sb[unit][:, t, :],
                 in_=y_sb[unit][:, t, :],
@@ -237,8 +237,7 @@ def tile_multiheadattention_pb_t_kernel(
                 scale=rstd[unit][:, t : t + 1],
             )
 
-        def shift_last(unit):
-            t = TILES - 1
+        def shift(unit, t):
             nc.gpsimd.tensor_tensor(
                 out=y_sb[unit][:, t, :], in0=y_sb[unit][:, t, :], in1=beta_sb[:], op=ALU.add
             )
@@ -349,6 +348,12 @@ def tile_multiheadattention_pb_t_kernel(
         for unit in range(UNITS + 1):
             ahead = unit + 2
             after = unit + 1
+            before = unit - 1
+            slices = [slice(0, TILES)]
+            if unit == UNITS - 1:
+                slices = [slice(t, t + 1) for t in range(TILES)]
+            offloaded = [t for t in range(TILES) if (before, t) in OFFLOADED]
+            kept = [t for t in range(TILES) if before >= 0 and t not in offloaded]
             if unit + LOADED < UNITS:
                 load(unit + LOADED)
             if ahead < UNITS:
@@ -358,13 +363,14 @@ def tile_multiheadattention_pb_t_kernel(
             if unit < UNITS:
                 add_residual(unit)
             if unit == 0:
-                average(unit)
+                average(unit, slices[0])
             if ahead < UNITS:
                 copy_tile(ahead, 0)
-            if unit - 1 in OFFLOADED:
-                scale_last(unit - 1)
+            for t in offloaded:
+                scale(before, t)
             if 0 < unit < UNITS:
-                average(unit)
+                for tiles in slices:
+                    average(unit, tiles)
             if ahead < UNITS:
                 copy_tile(ahead, 1)
             if unit < UNITS:
@@ -372,7 +378,8 @@ def tile_multiheadattention_pb_t_kernel(
             if ahead < UNITS:
                 copy_first_residual(ahead)
             if unit < UNITS:
-                invert_deviation(unit)
+                for tiles in slices:
+                    invert_deviation(unit, tiles)
             if after < UNITS:
                 quantise(after, 0, TILES)
                 for t in range(TILES):
@@ -382,11 +389,11 @@ def tile_multiheadattention_pb_t_kernel(
                 nc.vector.tensor_copy(out=beta_sb[:], in_=beta_bc)
             if ahead < UNITS:
                 add_residuals(ahead)
-            if unit - 1 in OFFLOADED:
-                shift_last(unit - 1)
-            if 0 <= unit - 1:
-                finish(unit - 1)
-            if unit - 1 in OFFLOADED:
-                store(unit - 1, TILES - 1, 1)
+            for t in offloaded:
+                shift(before, t)
+            for t in kept:
+                finish(before, t, 2 if (before, t) == (UNITS - 1, TILES - 1) else 1)
+            for t in offloaded:
+                store(before, t, slice(0, D))
             if unit < UNITS:
                 centre(unit)

@@ -43,8 +43,7 @@ def tile_multiheadattention_pb_t_kernel(
         w_pool = stack.enter_context(tc.tile_pool(name="w", bufs=W_TILES))
         heads_pool = stack.enter_context(tc.tile_pool(name="heads", bufs=LOADED))
         q_pool = stack.enter_context(tc.tile_pool(name="q", bufs=LOADED))
-        resid_pool = stack.enter_context(tc.tile_pool(name="resid", bufs=4))
-        grouped_pool = stack.enter_context(tc.tile_pool(name="grouped", bufs=3))
+        grouped_pool = stack.enter_context(tc.tile_pool(name="grouped", bufs=5))
         mx_pool = stack.enter_context(tc.tile_pool(name="mx", bufs=3))
         x_pool = stack.enter_context(tc.tile_pool(name="x", bufs=3))
         y_pool = stack.enter_context(tc.tile_pool(name="y", bufs=4))
@@ -99,7 +98,6 @@ def tile_multiheadattention_pb_t_kernel(
             return q_sb[unit][:].rearrange("p (t n) -> p t n", t=TILES)
 
         def sum_first_residual(unit):
-            resid[unit] = resid_pool.tile([P, TILES, D], F32, name="resid")
             if unit in HELPED:
                 bank = flip_psum.tile([P, D], F32, name="flipped")
                 nc.tensor.matmul(
@@ -109,6 +107,10 @@ def tile_multiheadattention_pb_t_kernel(
                     out=bank[:], lhsT=ones[:], rhs=vec_rows[:, 0:D], start=False, stop=True
                 )
                 total[unit] = bank
+
+        def place_residual(unit):
+            words = grouped[unit - 1][:].bitcast(F32)
+            resid[unit] = words.rearrange("p (t n) -> p t n", t=TILES)
 
         def copy_first_residual(unit):
             if unit in HELPED:
@@ -274,14 +276,15 @@ def tile_multiheadattention_pb_t_kernel(
         w_scales = const.tile([P, HEADS * D], U8, align_bytes=64)
         w_grouped = {}
 
-        halves = {}
-        for j in range(W_TILES):
-            halves[j] = w_pool.tile([P, HEADS, HALVES, P], F32, name="halves")
-            nc.vector.tensor_copy(out=halves[j][:], in_=w_words[:, j])
+        halves = {0: w_words[:, 0]}
+        for j in range(1, W_TILES):
+            sorted_words = w_pool.tile([P, HEADS, HALVES, P], F32, name="halves")
+            nc.vector.tensor_copy(out=sorted_words[:], in_=w_words[:, j])
+            halves[j] = sorted_words[:]
 
         def flip_weights(j):
             bank = acc_psum.tile([P, D], F32, name="acc")
-            flip_rows(bank, halves[j][:])
+            flip_rows(bank, halves[j])
             w_grouped[j] = w_pool.tile(
                 [P, HEADS * P * PACK], BF16, name="w_grouped", align_bytes=64
             )
@@ -324,14 +327,15 @@ def tile_multiheadattention_pb_t_kernel(
         copy_tile(0, 1)
         flip_tile(1, 0)
         copy_tile(1, 0)
-        resid[0] = resid_pool.tile([P, TILES, D], F32, name="resid")
+        first_resid = const.tile([P, TILES, D], F32)
+        resid[0] = first_resid[:]
         for t in range(TILES):
             quantise(0, t, 1)
             project(0, t)
             nc.vector.tensor_tensor(
                 out=resid[0][:, t, :], in0=q_rows(0)[:, t, :], in1=bias_ps[:], op=ALU.add
             )
-        bias_sb = const.tile([P, D], F32)
+        bias_sb = const.tile([P, D], BF16)
         nc.scalar.copy(out=bias_sb[:], in_=bias_ps[:])
         flip_tile(1, 1)
         copy_tile(1, 1)
@@ -342,7 +346,7 @@ def tile_multiheadattention_pb_t_kernel(
         broadcast(beta_bc, 2)
         beta_sb = const.tile([P, D], BF16)
         sum_first_residual(1)
-        wait_for_codes(0)
+        place_residual(1)
         add_residuals(1)
 
         for unit in range(UNITS + 1):
@@ -375,16 +379,18 @@ def tile_multiheadattention_pb_t_kernel(
                 copy_tile(ahead, 1)
             if unit < UNITS:
                 sum_squares(unit)
-            if ahead < UNITS:
-                copy_first_residual(ahead)
-            if unit < UNITS:
-                for tiles in slices:
-                    invert_deviation(unit, tiles)
             if after < UNITS:
                 quantise(after, 0, TILES)
                 for t in range(TILES):
                     project(after, t)
+            if ahead < UNITS:
+                place_residual(ahead)
+                copy_first_residual(ahead)
+            elif after < UNITS:
                 wait_for_codes(after)
+            if unit < UNITS:
+                for tiles in slices:
+                    invert_deviation(unit, tiles)
             if unit == 0:
                 nc.vector.tensor_copy(out=beta_sb[:], in_=beta_bc)
             if ahead < UNITS:

@@ -366,31 +366,29 @@ def tile_multiheadattention_pb_t_kernel(
                 sum_first_residual(ahead)
             if unit < UNITS:
                 add_residual(unit)
-            if unit == 0:
-                average(unit, slices[0])
-            if ahead < UNITS:
-                copy_tile(ahead, 0)
             for t in offloaded:
                 scale(before, t)
-            if 0 < unit < UNITS:
+            if unit < UNITS:
                 for tiles in slices:
                     average(unit, tiles)
             if ahead < UNITS:
-                copy_tile(ahead, 1)
+                copy_tile(ahead, 0)
             if unit < UNITS:
                 sum_squares(unit)
+            if ahead < UNITS:
+                copy_tile(ahead, 1)
             if after < UNITS:
-                quantise(after, 0, TILES)
                 for t in range(TILES):
+                    quantise(after, t, 1)
                     project(after, t)
+            if unit < UNITS:
+                for tiles in slices:
+                    invert_deviation(unit, tiles)
             if ahead < UNITS:
                 place_residual(ahead)
                 copy_first_residual(ahead)
             elif after < UNITS:
                 wait_for_codes(after)
-            if unit < UNITS:
-                for tiles in slices:
-                    invert_deviation(unit, tiles)
             if unit == 0:
                 nc.vector.tensor_copy(out=beta_sb[:], in_=beta_bc)
             if ahead < UNITS:

from contextlib import ExitStack

import concourse.mybir as mybir
from concourse.masks import make_identity

F32 = mybir.dt.float32
BF16 = mybir.dt.bfloat16
U32 = mybir.dt.uint32
U8 = mybir.dt.uint8
FP8X4 = mybir.dt.float8_e4m3fn_x4
ALU = mybir.AluOpType
ACT = mybir.ActivationFunctionType

P = 128
HEADS = 2
D = 512
ROWS = 4096
PACK = 4
HALVES = 2
TILES = 2
UNITS = ROWS // (P * TILES)
LOADED = 6
W_TILES = D // P
LN_EPS = 1e-5
HELPED = frozenset(range(3, UNITS)) - {UNITS // 2, 3 * UNITS // 4}
OFFLOADED = frozenset(
    (u, TILES - 1) for u in range(UNITS - 1) if u + 3 in HELPED or u + 3 >= UNITS
) | {(UNITS - 3, 0)}

FLOPS = 2 * ROWS * HEADS * D * D


def tile_multiheadattention_pb_t_kernel(
    tc, heads, q, proj_w, proj_b, ln_gamma, ln_beta, out
):
    nc = tc.nc
    heads_units = heads.rearrange("h (i p t) d -> i p h (t d)", p=P, t=TILES)
    q_units = q.flatten_outer_dims().rearrange("(i p t) d -> i p (t d)", p=P, t=TILES)
    out_units = out.flatten_outer_dims().rearrange("(i p t) d -> i p (t d)", p=P, t=TILES)

    with ExitStack() as stack:
        const = stack.enter_context(tc.tile_pool(name="const", bufs=1))
        w_pool = stack.enter_context(tc.tile_pool(name="w", bufs=W_TILES))
        heads_pool = stack.enter_context(tc.tile_pool(name="heads", bufs=LOADED))
        q_pool = stack.enter_context(tc.tile_pool(name="q", bufs=LOADED))
        grouped_pool = stack.enter_context(tc.tile_pool(name="grouped", bufs=5))
        mx_pool = stack.enter_context(tc.tile_pool(name="mx", bufs=3))
        x_pool = stack.enter_context(tc.tile_pool(name="x", bufs=3))
        y_pool = stack.enter_context(tc.tile_pool(name="y", bufs=4))
        scratch_pool = stack.enter_context(tc.tile_pool(name="scratch", bufs=4))
        stats_pool = stack.enter_context(tc.tile_pool(name="stats", bufs=4))
        affine_psum = stack.enter_context(tc.psum_pool(name="affine_psum", bufs=1))
        flip_psum = stack.enter_context(tc.psum_pool(name="flip_psum", bufs=3))
        acc_psum = stack.enter_context(tc.psum_pool(name="acc_psum", bufs=2 * TILES))
        stack.enter_context(tc.manual_schedule())

        heads_sb, q_sb, resid, flipped, grouped, codes, scales = {}, {}, {}, {}, {}, {}, {}
        total, acc, x_sb, y_sb = {}, {}, {}, {}
        row_sum, mean, sq_sum, rstd = {}, {}, {}, {}

        def load(unit):
            heads_sb[unit] = heads_pool.tile([P, HEADS, TILES * D], BF16, name="heads_sb")
            q_sb[unit] = q_pool.tile([P, TILES * D], BF16, name="q_sb")
            nc.sync.dma_start(out=heads_sb[unit][:], in_=heads_units[unit])
            nc.sync.dma_start(out=q_sb[unit][:], in_=q_units[unit])

        def flip_rows(flipped, src_words):
            planes = flipped[:].rearrange("p (h u r) -> p h u r", h=HEADS, u=HALVES)
            for h in range(HEADS):
                for u in range(HALVES):
                    nc.tensor.transpose(planes[:, h, u, :], src_words[:, h, u, :], ident[:])

        def copy_flipped(flipped, dst_words, copy):
            planes = flipped[:].rearrange("p (h u r) -> p h r u", h=HEADS, u=HALVES)
            copy(out=dst_words, in_=planes)

        def flip_tile(unit, t):
            src = (
                heads_sb[unit][:]
                .rearrange("p h x -> p (h x)")
                .bitcast(F32)
                .rearrange("p (h t w u) -> p h t u w", h=HEADS, t=TILES, u=HALVES)
            )
            flipped[unit, t] = flip_psum.tile([P, D], F32, name="flipped")
            flip_rows(flipped[unit, t], src[:, :, t])

        def copy_tile(unit, t):
            if t == 0:
                grouped[unit] = grouped_pool.tile(
                    [P, TILES * HEADS * P * PACK], BF16, name="grouped", align_bytes=64
                )
            dst = grouped[unit][:].bitcast(F32).rearrange(
                "p (t h r u) -> p t h r u", t=TILES, h=HEADS, u=HALVES
            )
            copy_flipped(flipped[unit, t], dst[:, t], nc.scalar.copy)

        def q_rows(unit):
            return q_sb[unit][:].rearrange("p (t n) -> p t n", t=TILES)

        def sum_first_residual(unit):
            if unit in HELPED:
                bank = flip_psum.tile([P, D], F32, name="flipped")
                nc.tensor.matmul(
                    out=bank[:], lhsT=ident_bf[:], rhs=q_rows(unit)[:, 0, :], start=True, stop=False
                )
                nc.tensor.matmul(
                    out=bank[:], lhsT=ones[:], rhs=vec_rows[:, 0:D], start=False, stop=True
                )
                total[unit] = bank

        def place_residual(unit):
            words = grouped[unit - 1][:].bitcast(F32)
            resid[unit] = words.rearrange("p (t n) -> p t n", t=TILES)

        def copy_first_residual(unit):
            if unit in HELPED:
                nc.scalar.copy(out=resid[unit][:, 0, :], in_=total[unit][:])

        def add_residuals(unit):
            first = 1 if unit in HELPED else 0
            nc.gpsimd.tensor_tensor(
                out=resid[unit][:, first:, :],
                in0=q_rows(unit)[:, first:, :],
                in1=bias_sb[:].unsqueeze(1).to_broadcast([P, TILES - first, D]),
                op=ALU.add,
            )

        def wait_for_codes(unit):
            gate = stats_pool.tile([P, 1], U32, name="gate")
            last = TILES * HEADS * P - 1
            nc.gpsimd.tensor_copy(out=gate[:], in_=codes[unit][:, last : last + 1])

        def quantise(unit, first, count):
            width = HEADS * P
            if first == 0:
                codes[unit] = mx_pool.tile([P, TILES * width], U32, name="codes", align_bytes=64)
                scales[unit] = mx_pool.tile([P, TILES * width], U8, name="scales", align_bytes=64)
            cols = slice(first * width, (first + count) * width)
            nc.vector.quantize_mx(
                out=codes[unit][:, cols].bitcast(FP8X4),
                scales=scales[unit][:, cols],
                in_=grouped[unit][:, first * width * PACK : (first + count) * width * PACK],
            )

        def project(unit, t):
            acc[unit, t] = acc_psum.tile([P, D], F32, name="acc")
            for h in range(HEADS):
                rows = slice((t * HEADS + h) * P, (t * HEADS + h + 1) * P)
                cols = slice(h * D, (h + 1) * D)
                nc.tensor.matmul_mx(
                    out=acc[unit, t][:],
                    lhsT=codes[unit][:, rows].bitcast(FP8X4),
                    lhsT_scale=scales[unit][:, rows],
                    rhs=w_codes[:, cols].bitcast(FP8X4),
                    rhs_scale=w_scales[:, cols],
                    start=(h == 0),
                    stop=(h == HEADS - 1),
                )

        def add_residual(unit):
            x_sb[unit] = x_pool.tile([P, TILES, D], F32, name="x_sb")
            row_sum[unit] = stats_pool.tile([P, TILES], F32, name="row_sum")
            for t in range(TILES):
                nc.vector.scalar_tensor_tensor(
                    out=x_sb[unit][:, t, :],
                    in0=acc[unit, t][:],
                    scalar=1.0,
                    in1=resid[unit][:, t, :],
                    op0=ALU.mult,
                    op1=ALU.add,
                    accum_out=row_sum[unit][:, t : t + 1],
                )

        def average(unit, tiles):
            if tiles.start == 0:
                mean[unit] = stats_pool.tile([P, TILES], F32, name="mean")
            nc.scalar.mul(out=mean[unit][:, tiles], in_=row_sum[unit][:, tiles], mul=1.0 / D)

        def sum_squares(unit):
            sq_sum[unit] = stats_pool.tile([P, TILES], F32, name="sq_sum")
            for t in range(TILES):
                squares = scratch_pool.tile([P, D], BF16, name="squares")
                nc.scalar.activation(
                    out=squares[:],
                    in_=x_sb[unit][:, t, :],
                    func=ACT.Square,
                    bias=mean[unit][:, t : t + 1],
                    scale=-1.0,
                    accum_out=sq_sum[unit][:, t : t + 1],
                )

        def invert_deviation(unit, tiles):
            if tiles.start == 0:
                rstd[unit] = stats_pool.tile([P, TILES], F32, name="rstd")
            nc.scalar.activation(
                out=rstd[unit][:, tiles],
                in_=sq_sum[unit][:, tiles],
                func=ACT.Abs_reciprocal_sqrt,
                bias=eps[:],
                scale=1.0 / D,
            )

        def centre(unit):
            y_sb[unit] = y_pool.tile([P, TILES, D], F32, name="y_sb")
            for t in range(TILES):
                nc.vector.scalar_tensor_tensor(
                    out=y_sb[unit][:, t, :],
                    in0=x_sb[unit][:, t, :],
                    scalar=mean[unit][:, t : t + 1],
                    in1=gamma_bc,
                    op0=ALU.subtract,
                    op1=ALU.mult,
                )

        def store(unit, t, cols):
            nc.sync.dma_start(
                out=out_units[unit][:, t * D + cols.start : t * D + cols.stop],
                in_=y_sb[unit][:, t, cols],
            )

        def finish(unit, t, pieces):
            for piece in range(pieces):
                cols = slice(piece * D // pieces, (piece + 1) * D // pieces)
                nc.vector.scalar_tensor_tensor(
                    out=y_sb[unit][:, t, cols],
                    in0=y_sb[unit][:, t, cols],
                    scalar=rstd[unit][:, t : t + 1],
                    in1=beta_bc[:, cols],
                    op0=ALU.mult,
                    op1=ALU.add,
                )
                store(unit, t, cols)

        def scale(unit, t):
            nc.scalar.activation(
                out=y_sb[unit][:, t, :],
                in_=y_sb[unit][:, t, :],
                func=ACT.Copy,
                scale=rstd[unit][:, t : t + 1],
            )

        def shift(unit, t):
            nc.gpsimd.tensor_tensor(
                out=y_sb[unit][:, t, :], in0=y_sb[unit][:, t, :], in1=beta_sb[:], op=ALU.add
            )

        vec_rows = const.tile([P, 3 * D], BF16)
        nc.gpsimd.memset(vec_rows[:].bitcast(F32), 0.0)
        ident = const.tile([P, P], F32)
        make_identity(nc, ident[:])
        ones = const.tile([P, P], BF16)
        nc.vector.memset(ones[:], 1.0)
        eps = const.tile([P, 1], F32)
        nc.vector.memset(eps[:], LN_EPS)
        ident_bf = const.tile([P, P], BF16)
        nc.vector.tensor_copy(out=ident_bf[:], in_=ident[:])

        for i, vec in enumerate((proj_b, ln_gamma, ln_beta)):
            nc.scalar.dma_start(out=vec_rows[0:1, i * D : (i + 1) * D], in_=vec.unsqueeze(0))
        w_raw = const.tile([P, W_TILES, HEADS * D], BF16)
        w_rows = proj_w.rearrange("(j p) k -> p j k", p=P)
        for j in range(W_TILES):
            nc.sync.dma_start(out=w_raw[:, j, :], in_=w_rows[:, j, :])
        for unit in range(LOADED):
            load(unit)
        warm = const.tile([P, 1], F32)
        nc.scalar.activation(out=warm[:], in_=eps[:], func=ACT.Abs_reciprocal_sqrt)

        w_words = (
            w_raw[:]
            .rearrange("p j k -> p (j k)")
            .bitcast(F32)
            .rearrange("p (j h w u) -> p j h u w", j=W_TILES, h=HEADS, u=HALVES)
        )
        w_codes = const.tile([P, HEADS * D], U32, align_bytes=64)
        w_scales = const.tile([P, HEADS * D], U8, align_bytes=64)
        w_grouped = {}

        halves = {0: w_words[:, 0]}
        for j in range(1, W_TILES):
            sorted_words = w_pool.tile([P, HEADS, HALVES, P], F32, name="halves")
            nc.vector.tensor_copy(out=sorted_words[:], in_=w_words[:, j])
            halves[j] = sorted_words[:]

        def flip_weights(j):
            bank = acc_psum.tile([P, D], F32, name="acc")
            flip_rows(bank, halves[j])
            w_grouped[j] = w_pool.tile(
                [P, HEADS * P * PACK], BF16, name="w_grouped", align_bytes=64
            )
            dst = w_grouped[j][:].bitcast(F32).rearrange(
                "p (h n u) -> p h n u", h=HEADS, u=HALVES
            )
            copy_flipped(bank, dst, nc.vector.tensor_copy if j % 2 else nc.scalar.copy)

        def quantise_weights(j):
            for h in range(HEADS):
                cols = slice(h * D + j * P, h * D + (j + 1) * P)
                nc.vector.quantize_mx(
                    out=w_codes[:, cols].bitcast(FP8X4),
                    scales=w_scales[:, cols],
                    in_=w_grouped[j][:, h * P * PACK : (h + 1) * P * PACK],
                )

        def broadcast(bank, i):
            nc.tensor.matmul(
                out=bank,
                lhsT=ones[:],
                rhs=vec_rows[:, i * D : (i + 1) * D],
                start=True,
                stop=True,
            )

        flip_weights(0)
        flip_weights(1)
        quantise_weights(0)
        quantise_weights(1)
        flip_weights(2)
        flip_weights(3)
        quantise_weights(2)
        quantise_weights(3)
        flip_tile(0, 0)
        copy_tile(0, 0)
        bias_ps = acc_psum.tile([P, D], F32, name="acc")
        broadcast(bias_ps[:], 0)
        flip_tile(0, 1)
        copy_tile(0, 1)
        flip_tile(1, 0)
        copy_tile(1, 0)
        first_resid = const.tile([P, TILES, D], F32)
        resid[0] = first_resid[:]
        for t in range(TILES):
            quantise(0, t, 1)
            project(0, t)
            nc.vector.tensor_tensor(
                out=resid[0][:, t, :], in0=q_rows(0)[:, t, :], in1=bias_ps[:], op=ALU.add
            )
        bias_sb = const.tile([P, D], BF16)
        nc.scalar.copy(out=bias_sb[:], in_=bias_ps[:])
        flip_tile(1, 1)
        copy_tile(1, 1)
        affine = affine_psum.tile([P, 2 * D], BF16)
        gamma_bc = affine[:, 0:D]
        beta_bc = affine[:, D : 2 * D]
        broadcast(gamma_bc, 1)
        broadcast(beta_bc, 2)
        beta_sb = const.tile([P, D], BF16)
        sum_first_residual(1)
        place_residual(1)
        add_residuals(1)

        for unit in range(UNITS + 1):
            ahead = unit + 2
            after = unit + 1
            before = unit - 1
            slices = [slice(0, TILES)]
            if unit == UNITS - 1:
                slices = [slice(t, t + 1) for t in range(TILES)]
            offloaded = [t for t in range(TILES) if (before, t) in OFFLOADED]
            kept = [t for t in range(TILES) if before >= 0 and t not in offloaded]
            if unit + LOADED < UNITS:
                load(unit + LOADED)
            if ahead < UNITS:
                for t in range(TILES):
                    flip_tile(ahead, t)
                sum_first_residual(ahead)
            if unit < UNITS:
                add_residual(unit)
            for t in offloaded:
                scale(before, t)
            if unit < UNITS:
                for tiles in slices:
                    average(unit, tiles)
            if ahead < UNITS:
                copy_tile(ahead, 0)
            if unit < UNITS:
                sum_squares(unit)
            if ahead < UNITS:
                copy_tile(ahead, 1)
            if after < UNITS:
                for t in range(TILES):
                    quantise(after, t, 1)
                    project(after, t)
            if unit < UNITS:
                for tiles in slices:
                    invert_deviation(unit, tiles)
            if ahead < UNITS:
                place_residual(ahead)
                copy_first_residual(ahead)
            elif after < UNITS:
                wait_for_codes(after)
            if unit == 0:
                nc.vector.tensor_copy(out=beta_sb[:], in_=beta_bc)
            if ahead < UNITS:
                add_residuals(ahead)
            for t in offloaded:
                shift(before, t)
            for t in kept:
                finish(before, t, 2 if (before, t) == (UNITS - 1, TILES - 1) else 1)
            for t in offloaded:
                store(before, t, slice(0, D))
            if unit < UNITS:
                centre(unit)
